import numpy as np
import ml_dtypes


def mxq(x, axis, fmt="e4m3"):
    dtype, down = {"e4m3": (ml_dtypes.float8_e4m3fn, 7), "e5m2": (ml_dtypes.float8_e5m2, 14)}[fmt]
    v = np.moveaxis(np.asarray(x, np.float32).astype(ml_dtypes.bfloat16).astype(np.float64), axis, -1)
    blocks = v.reshape(v.shape[:-1] + (-1, 32))
    amax = np.abs(blocks).max(-1, keepdims=True)
    byte = np.maximum(np.where(amax > 0, np.frexp(amax)[1] - 1 + 127, 0) - down, 1)
    scale = np.exp2(byte - 127.0)
    codes = (blocks / scale).astype(np.float32).astype(dtype).astype(np.float64)
    return np.moveaxis((codes * scale).reshape(v.shape), -1, axis)


WIDE = False


def mx_kscale(k):
    if not WIDE:
        return np.ones(k)
    levels = np.array([10, -10, 5, -5, 0])
    if k % 512:
        return np.exp2(np.random.permutation(np.resize(levels, k // 32))).repeat(32)
    a = np.empty((k // 512, 16))
    for p in range(k // 512):
        a[p, :8] = np.random.permutation(np.resize(levels, 8))
        for g in range(8):
            far = levels[np.abs(levels - a[p, g]) >= 10]
            a[p, g + 8] = far[np.random.randint(len(far))]
    return np.exp2(a.ravel()).repeat(32)


BF16 = ml_dtypes.bfloat16


def bf(x):
    return np.asarray(x, np.float32).astype(BF16)


def f64(x):
    return np.asarray(x).astype(np.float64)


B, NV, NH, NT = 16384, 1024, 128, 2


def softplus(v):
    return np.logaddexp(v, 0.0)


def softmax_last(v):
    e = np.exp(v - v.max(axis=1, keepdims=True))
    return e / e.sum(axis=1, keepdims=True)


def setup_inputs():
    s = mx_kscale(NV)
    return {"input_data": bf(np.random.standard_normal((B, NV)) * s),
            "W": bf(np.random.standard_normal((NH, NV)) / np.sqrt(NV) / s[None, :]),
            "U": bf(np.random.standard_normal((NH, NT)) * 0.5),
            "h_bias": bf(np.random.standard_normal((1, NH)) * 0.5 - np.log(NH / 16.0)),
            "y_bias": bf(np.random.standard_normal((1, NT)) * 0.5)}


def reference(input_data, W, U, h_bias, y_bias):
    pf = (mxq(f64(input_data), 1, "e4m3") @ mxq(f64(W), 1, "e4m3").T) + f64(h_bias)
    sp = softplus(pf[:, :, None] + f64(U)[None, :, :])
    logits = f64(y_bias) + sp.sum(axis=1)
    return softmax_last(logits)

@@ -1,0 +1,245 @@
+from contextlib import ExitStack
+
+import concourse.mybir as mybir
+from concourse.masks import make_identity
+
+F32 = mybir.dt.float32
+BF16 = mybir.dt.bfloat16
+U32 = mybir.dt.uint32
+U8 = mybir.dt.uint8
+FP8X4 = mybir.dt.float8_e4m3fn_x4
+ACT = mybir.ActivationFunctionType
+ALU = mybir.AluOpType
+AX = mybir.AxisListType
+
+P = 128
+B, NV, NH = 16384, 1024, 128
+T_ALL = B // P
+T_GRP = 4
+NG = T_ALL // T_GRP
+COLS = T_GRP * P
+PASSES = NV // 512
+HALF = NH // 2
+XBUFS = 8
+T_EARLY = 112
+FLOPS = 2 * B * NV * NH
+
+
+def tile_rbm_t_kernel(tc, input_data, W, U, h_bias, y_bias, out):
+    nc = tc.nc
+    with ExitStack() as ctx:
+        keep = ctx.enter_context(tc.tile_pool(name="keep", bufs=1))
+        xpool = ctx.enter_context(tc.tile_pool(name="xpool", bufs=XBUFS))
+        gpool = ctx.enter_context(tc.tile_pool(name="gpool", bufs=3))
+        qpool = ctx.enter_context(tc.tile_pool(name="qpool", bufs=4))
+        tpool = ctx.enter_context(tc.tile_pool(name="tpool", bufs=4))
+        ps_xt = ctx.enter_context(tc.psum_pool(name="ps_xt", bufs=4))
+        ps_pf = ctx.enter_context(tc.psum_pool(name="ps_pf", bufs=2))
+        ps_rt = ctx.enter_context(tc.psum_pool(name="ps_rt", bufs=2))
+        ctx.enter_context(tc.manual_schedule())
+
+        xv = input_data.rearrange("(p t) k -> p (t k)", t=T_ALL)
+        xin_t, xt_t, grp_t, codes_t, scl_t, pf_t, th_t, rt_t = {}, {}, {}, {}, {}, {}, {}, {}
+
+        def load(g):
+            if g >= NG:
+                return
+            xin = xpool.tile([P, T_GRP * NV], BF16)
+            xin_t[g] = xin
+            pieces = T_GRP if g == 0 else 1
+            step = T_GRP * NV // pieces
+            for i in range(pieces):
+                nc.sync.dma_start(
+                    out=xin[:, i * step : (i + 1) * step],
+                    in_=xv[:, g * T_GRP * NV + i * step : g * T_GRP * NV + (i + 1) * step],
+                )
+
+        load(0)
+        wsb = keep.tile([P, NV], BF16)
+        nc.scalar.dma_start(out=wsb[:], in_=W)
+        usb = keep.tile([P, 2], BF16)
+        hsb = keep.tile([P, 1], BF16)
+        ysb = keep.tile([P, 2], BF16)
+        nc.vector.memset(ysb[:], 0.0)
+        with nc.allow_non_contiguous_dma(reason="one or two elements a partition"):
+            nc.scalar.dma_start(out=usb[:], in_=U)
+            nc.scalar.dma_start(out=hsb[:], in_=h_bias.rearrange("o j -> j o"))
+            nc.scalar.dma_start(out=ysb[0:1, :], in_=y_bias)
+        for g in range(1, XBUFS):
+            load(g)
+
+        ident = keep.tile([P, P], F32)
+        make_identity(nc, ident[:])
+
+        wgrp = keep.tile([P, PASSES * P * 4], BF16, align_bytes=64)
+        wcodes = keep.tile([P, PASSES * P], U32, align_bytes=64)
+        wscl = keep.tile([P, PASSES * P], U8, align_bytes=64)
+        tb = keep.tile([P, 1], F32)
+        usw = keep.tile([P, 2], F32)
+        ein = keep.tile([P, 2], F32)
+        eout = keep.tile([P, 2], F32)
+        ab = keep.tile([P, 2], F32)
+        prod = keep.tile([P, T_ALL, 2], F32)
+        ssum = keep.tile([P, T_ALL], F32)
+        rsum = keep.tile([P, T_ALL], F32)
+        osb = keep.tile([P, T_ALL, 2], F32)
+
+        def w_transposes():
+            ww = wsb[:].bitcast(F32)
+            wt = ps_rt.tile([P, PASSES, 2, P], F32, tag="rT")
+            rt_t["w"] = wt
+            for gp in range(PASSES):
+                for u in range(2):
+                    w0 = 256 * gp
+                    nc.tensor.transpose(out=wt[:, gp, u, :], in_=ww[:, w0 + u : w0 + 256 : 2], identity=ident[:])
+
+        def w_quantise():
+            nc.vector.tensor_copy(
+                out=wgrp[:].bitcast(F32).rearrange("p (g j u) -> p g j u", g=PASSES, u=2),
+                in_=rt_t["w"][:].rearrange("p g u j -> p g j u"),
+            )
+            nc.vector.quantize_mx(out=wcodes[:].bitcast(FP8X4), scales=wscl[:], in_=wgrp[:])
+
+        def constants_before_exp():
+            nc.vector.tensor_copy(out=usw[0:HALF, 0:1], in_=usb[0:HALF, 1:2])
+            nc.vector.tensor_copy(out=usw[0:HALF, 1:2], in_=usb[0:HALF, 0:1])
+            nc.vector.tensor_copy(out=usw[HALF:P, :], in_=usb[HALF:P, :])
+            nc.vector.tensor_tensor(out=tb[:], in0=hsb[:], in1=usw[:, 0:1], op=ALU.add)
+            nc.vector.tensor_scalar_mul(out=tb[:], in0=tb[:], scalar1=0.5)
+            nc.vector.tensor_tensor(out=ein[:, 0:1], in0=ysb[:, 0:1], in1=ysb[:, 1:2], op=ALU.subtract)
+            nc.vector.tensor_tensor(out=ein[:, 1:2], in0=usw[:, 1:2], in1=usw[:, 0:1], op=ALU.subtract)
+            nc.vector.tensor_tensor(out=ein[:, 1:2], in0=ein[:, 1:2], in1=ein[:, 0:1], op=ALU.add)
+
+        def constants_after_exp():
+            nc.vector.tensor_tensor(out=ab[:, 0:1], in0=eout[:, 1:2], in1=eout[:, 0:1], op=ALU.add)
+            nc.vector.tensor_tensor(out=ab[:, 1:2], in0=eout[:, 1:2], in1=eout[:, 0:1], op=ALU.subtract)
+            nc.vector.tensor_scalar_mul(out=ab[:], in0=ab[:], scalar1=0.5)
+
+        def on_vector(g, b):
+            return b == 3 and g % 4 != 0
+
+        def x_transposes(g, b):
+            if g < 0 or g >= NG:
+                return
+            gp, h = b // 2, b % 2
+            xw = xin_t[g][:].bitcast(F32)
+            xt = ps_xt.tile([P, 2, 256], F32)
+            xt_t[(g, b)] = xt
+            for tt in range(2):
+                for u in range(2):
+                    w0 = (2 * h + tt) * 512 + 256 * gp
+                    nc.tensor.transpose(
+                        out=xt[:, u, tt * P : (tt + 1) * P], in_=xw[:, w0 + u : w0 + 256 : 2], identity=ident[:]
+                    )
+
+        def copy_out(g, b):
+            if g < 0 or g >= NG:
+                return
+            if b == 0:
+                grp = gpool.tile([P, PASSES * COLS * 4], BF16, align_bytes=64)
+                grp_t[g] = grp
+            o0 = (b // 2) * 1024 + (b % 2) * 512
+            dst = grp_t[g][:].bitcast(F32)[:, o0 : o0 + 512].rearrange("p (c u) -> p c u", u=2)
+            src = xt_t[(g, b)][:].rearrange("p u c -> p c u")
+            if on_vector(g, b):
+                nc.vector.tensor_copy(out=dst, in_=src)
+            else:
+                nc.scalar.copy(out=dst, in_=src)
+
+        def quantise(g):
+            if g < 0 or g >= NG:
+                return
+            codes = qpool.tile([P, PASSES * COLS], U32, align_bytes=64)
+            scl = qpool.tile([P, PASSES * COLS], U8, align_bytes=64)
+            codes_t[g], scl_t[g] = codes, scl
+            nc.vector.quantize_mx(out=codes[:].bitcast(FP8X4), scales=scl[:], in_=grp_t[g][:])
+
+        def mx(g):
+            if g < 0 or g >= NG:
+                return
+            pf = ps_pf.tile([P, COLS], F32)
+            pf_t[g] = pf
+            for gp in range(PASSES):
+                nc.tensor.matmul_mx(
+                    out=pf[:],
+                    lhsT=wcodes[:, gp * P : (gp + 1) * P].bitcast(FP8X4),
+                    lhsT_scale=wscl[:, gp * P : (gp + 1) * P],
+                    rhs=codes_t[g][:, gp * COLS : (gp + 1) * COLS].bitcast(FP8X4),
+                    rhs_scale=scl_t[g][:, gp * COLS : (gp + 1) * COLS],
+                    start=(gp == 0),
+                    stop=(gp == PASSES - 1),
+                )
+
+        def tanh(g):
+            if g < 0 or g >= NG:
+                return
+            th = tpool.tile([P, COLS], F32)
+            th_t[g] = th
+            nc.scalar.activation(out=th[:], in_=pf_t[g][:], func=ACT.Tanh, bias=tb[:, 0:1], scale=0.5)
+
+        def affine(g):
+            if g < 0 or g >= NG:
+                return
+            nc.gpsimd.tensor_scalar(
+                out=th_t[g][:], in0=th_t[g][:], scalar1=ab[:, 1:2], scalar2=ab[:, 0:1], op0=ALU.mult, op1=ALU.add
+            )
+
+        def r_transposes(g):
+            if g < 0 or g >= NG:
+                return
+            rT = ps_rt.tile([P, T_GRP, P], F32)
+            rt_t[g] = rT
+            for tt in range(T_GRP):
+                nc.tensor.transpose(out=rT[:, tt, :], in_=th_t[g][:, tt * P : (tt + 1) * P], identity=ident[:])
+
+        def products(g):
+            if g < 0 or g >= NG:
+                return
+            nc.vector.tensor_reduce(
+                out=prod[:, g * T_GRP : (g + 1) * T_GRP, :].rearrange("p t s -> p (t s)"),
+                in_=rt_t[g][:].rearrange("p t (s j) -> p (t s) j", s=2),
+                axis=AX.X,
+                op=ALU.mult,
+            )
+
+        def normalise(t0, t1):
+            nc.vector.tensor_reduce(out=ssum[:, t0:t1], in_=prod[:, t0:t1, :], axis=AX.X, op=ALU.add)
+            nc.vector.reciprocal(out=rsum[:, t0:t1], in_=ssum[:, t0:t1])
+            nc.vector.tensor_tensor(
+                out=osb[:, t0:t1, :],
+                in0=prod[:, t0:t1, :],
+                in1=rsum[:, t0:t1].unsqueeze(2).to_broadcast([P, t1 - t0, 2]),
+                op=ALU.mult,
+            )
+
+        for s in range(NG + 5):
+            for b in range(4):
+                x_transposes(s, b)
+            if s == 0:
+                w_transposes()
+            load(s + XBUFS)
+            r_transposes(s - 4)
+            mx(s - 2)
+
+            if s == 0:
+                w_quantise()
+                constants_before_exp()
+            if s == 2:
+                nc.scalar.activation(out=eout[:], in_=ein[:], func=ACT.Exp)
+            tanh(s - 3)
+            for b in range(3):
+                copy_out(s, b)
+            if not on_vector(s, 3):
+                copy_out(s, 3)
+
+            products(s - 5)
+            quantise(s - 1)
+            if s == 2:
+                constants_after_exp()
+            affine(s - 3)
+            if on_vector(s, 3):
+                copy_out(s, 3)
+            if s == NG + 1:
+                normalise(0, T_EARLY)
+        normalise(T_EARLY, T_ALL)
+        nc.sync.dma_start(out=out.rearrange("(p t) c -> p (t c)", t=T_ALL), in_=osb[:].rearrange("p t c -> p (t c)"))

@@ -22,6 +22,7 @@ PASSES = NV // 512
 HALF = NH // 2
 XBUFS = 8
 T_EARLY = 112
+N_SPLIT = 2
 FLOPS = 2 * B * NV * NH
 
 
@@ -30,6 +31,7 @@ def tile_rbm_t_kernel(tc, input_data, W, U, h_bias, y_bias, out):
     with ExitStack() as ctx:
         keep = ctx.enter_context(tc.tile_pool(name="keep", bufs=1))
         xpool = ctx.enter_context(tc.tile_pool(name="xpool", bufs=XBUFS))
+        spool = ctx.enter_context(tc.tile_pool(name="spool", bufs=3))
         gpool = ctx.enter_context(tc.tile_pool(name="gpool", bufs=3))
         qpool = ctx.enter_context(tc.tile_pool(name="qpool", bufs=4))
         tpool = ctx.enter_context(tc.tile_pool(name="tpool", bufs=4))
@@ -39,6 +41,7 @@ def tile_rbm_t_kernel(tc, input_data, W, U, h_bias, y_bias, out):
         ctx.enter_context(tc.manual_schedule())
 
         xv = input_data.rearrange("(p t) k -> p (t k)", t=T_ALL)
+        sep_t = {}
         xin_t, xt_t, grp_t, codes_t, scl_t, pf_t, th_t, rt_t = {}, {}, {}, {}, {}, {}, {}, {}
 
         def load(g):
@@ -116,7 +119,15 @@ def tile_rbm_t_kernel(tc, input_data, W, U, h_bias, y_bias, out):
             nc.vector.tensor_scalar_mul(out=ab[:], in0=ab[:], scalar1=0.5)
 
         def on_vector(g, b):
-            return b == 3 and g % 4 != 0
+            return False
+
+        def separate(g):
+            if g < 1 or g >= NG:
+                return
+            sep = spool.tile([P, 2, N_SPLIT * 256], F32)
+            sep_t[g] = sep
+            src = xin_t[g][:].bitcast(F32)[:, 0 : N_SPLIT * 512]
+            nc.vector.tensor_copy(out=sep[:], in_=src.rearrange("p (b u) -> p u b", u=2))
 
         def x_transposes(g, b):
             if g < 0 or g >= NG:
@@ -127,10 +138,13 @@ def tile_rbm_t_kernel(tc, input_data, W, U, h_bias, y_bias, out):
             xt_t[(g, b)] = xt
             for tt in range(2):
                 for u in range(2):
-                    w0 = (2 * h + tt) * 512 + 256 * gp
-                    nc.tensor.transpose(
-                        out=xt[:, u, tt * P : (tt + 1) * P], in_=xw[:, w0 + u : w0 + 256 : 2], identity=ident[:]
-                    )
+                    t = 2 * h + tt
+                    if g > 0 and t < N_SPLIT:
+                        win = sep_t[g][:, u, t * 256 + gp * 128 : t * 256 + gp * 128 + 128]
+                    else:
+                        w0 = t * 512 + 256 * gp
+                        win = xw[:, w0 + u : w0 + 256 : 2]
+                    nc.tensor.transpose(out=xt[:, u, tt * P : (tt + 1) * P], in_=win, identity=ident[:])
 
         def copy_out(g, b):
             if g < 0 or g >= NG:
@@ -180,7 +194,7 @@ def tile_rbm_t_kernel(tc, input_data, W, U, h_bias, y_bias, out):
         def affine(g):
             if g < 0 or g >= NG:
                 return
-            nc.gpsimd.tensor_scalar(
+            nc.vector.tensor_scalar(
                 out=th_t[g][:], in0=th_t[g][:], scalar1=ab[:, 1:2], scalar2=ab[:, 0:1], op0=ALU.mult, op1=ALU.add
             )
 
@@ -232,6 +246,7 @@ def tile_rbm_t_kernel(tc, input_data, W, U, h_bias, y_bias, out):
             if not on_vector(s, 3):
                 copy_out(s, 3)
 
+            separate(s + 1)
             products(s - 5)
             quantise(s - 1)
             if s == 2:

@@ -21,8 +21,8 @@ COLS = T_GRP * P
 PASSES = NV // 512
 HALF = NH // 2
 XBUFS = 8
-T_EARLY = 112
-N_SPLIT = 2
+T_EARLY = 100
+FIRST_SEPARATED = 3
 FLOPS = 2 * B * NV * NH
 
 
@@ -119,14 +119,18 @@ def tile_rbm_t_kernel(tc, input_data, W, U, h_bias, y_bias, out):
             nc.vector.tensor_scalar_mul(out=ab[:], in0=ab[:], scalar1=0.5)
 
         def on_vector(g, b):
-            return False
+            return (g == 0 and b in (1, 3)) or (g == 1 and b in (1, 3))
+
+        def n_separated(g):
+            return 2 if g >= FIRST_SEPARATED else 0
 
         def separate(g):
-            if g < 1 or g >= NG:
+            if g < FIRST_SEPARATED or g >= NG:
                 return
-            sep = spool.tile([P, 2, N_SPLIT * 256], F32)
+            n = n_separated(g)
+            sep = spool.tile([P, 2, n * 256], F32, name="sep%d" % n)
             sep_t[g] = sep
-            src = xin_t[g][:].bitcast(F32)[:, 0 : N_SPLIT * 512]
+            src = xin_t[g][:].bitcast(F32)[:, 0 : n * 512]
             nc.vector.tensor_copy(out=sep[:], in_=src.rearrange("p (b u) -> p u b", u=2))
 
         def x_transposes(g, b):
@@ -139,7 +143,7 @@ def tile_rbm_t_kernel(tc, input_data, W, U, h_bias, y_bias, out):
             for tt in range(2):
                 for u in range(2):
                     t = 2 * h + tt
-                    if g > 0 and t < N_SPLIT:
+                    if t < n_separated(g):
                         win = sep_t[g][:, u, t * 256 + gp * 128 : t * 256 + gp * 128 + 128]
                     else:
                         w0 = t * 512 + 256 * gp
@@ -149,7 +153,7 @@ def tile_rbm_t_kernel(tc, input_data, W, U, h_bias, y_bias, out):
         def copy_out(g, b):
             if g < 0 or g >= NG:
                 return
-            if b == 0:
+            if g not in grp_t:
                 grp = gpool.tile([P, PASSES * COLS * 4], BF16, align_bytes=64)
                 grp_t[g] = grp
             o0 = (b // 2) * 1024 + (b % 2) * 512
@@ -163,10 +167,60 @@ def tile_rbm_t_kernel(tc, input_data, W, U, h_bias, y_bias, out):
         def quantise(g):
             if g < 0 or g >= NG:
                 return
+            new_codes(g)
+            nc.vector.quantize_mx(out=codes_t[g][:].bitcast(FP8X4), scales=scl_t[g][:], in_=grp_t[g][:])
+
+        def new_codes(g):
             codes = qpool.tile([P, PASSES * COLS], U32, align_bytes=64)
             scl = qpool.tile([P, PASSES * COLS], U8, align_bytes=64)
             codes_t[g], scl_t[g] = codes, scl
-            nc.vector.quantize_mx(out=codes[:].bitcast(FP8X4), scales=scl[:], in_=grp_t[g][:])
+
+        def quantise_bank(g, b):
+            c0 = (b // 2) * COLS + (b % 2) * 256
+            nc.vector.quantize_mx(
+                out=codes_t[g][:, c0 : c0 + 256].bitcast(FP8X4),
+                scales=scl_t[g][:, c0 : c0 + 256],
+                in_=grp_t[g][:, 4 * c0 : 4 * c0 + 1024],
+            )
+
+        def mx_half(g, h, pf):
+            pf_t[(g, h)] = pf
+            for gp in range(PASSES):
+                c0 = gp * COLS + h * 256
+                nc.tensor.matmul_mx(
+                    out=pf,
+                    lhsT=wcodes[:, gp * P : (gp + 1) * P].bitcast(FP8X4),
+                    lhsT_scale=wscl[:, gp * P : (gp + 1) * P],
+                    rhs=codes_t[g][:, c0 : c0 + 256].bitcast(FP8X4),
+                    rhs_scale=scl_t[g][:, c0 : c0 + 256],
+                    start=(gp == 0),
+                    stop=(gp == PASSES - 1),
+                )
+
+        def tanh_half(g, h):
+            th = tpool.tile([P, 256], F32)
+            th_t[(g, h)] = th
+            nc.scalar.activation(out=th[:], in_=pf_t[(g, h)], func=ACT.Tanh, bias=tb[:, 0:1], scale=0.5)
+
+        def affine_scalar(k):
+            nc.scalar.activation(
+                out=th_t[k][:], in_=th_t[k][:], func=ACT.Identity, bias=ab[:, 0:1], scale=ab[:, 1:2]
+            )
+
+        def r_half(g, h):
+            rT = ps_rt.tile([P, 2, P], F32, tag="rT")
+            rt_t[(g, h)] = rT
+            for tt in range(2):
+                nc.tensor.transpose(out=rT[:, tt, :], in_=th_t[(g, h)][:, tt * P : (tt + 1) * P], identity=ident[:])
+
+        def products_half(g, h):
+            t0 = g * T_GRP + 2 * h
+            nc.vector.tensor_reduce(
+                out=prod[:, t0 : t0 + 2, :].rearrange("p t s -> p (t s)"),
+                in_=rt_t[(g, h)][:].rearrange("p t (s j) -> p (t s) j", s=2),
+                axis=AX.X,
+                op=ALU.mult,
+            )
 
         def mx(g):
             if g < 0 or g >= NG:
@@ -192,7 +246,7 @@ def tile_rbm_t_kernel(tc, input_data, W, U, h_bias, y_bias, out):
             nc.scalar.activation(out=th[:], in_=pf_t[g][:], func=ACT.Tanh, bias=tb[:, 0:1], scale=0.5)
 
         def affine(g):
-            if g < 0 or g >= NG:
+            if g not in th_t:
                 return
             nc.vector.tensor_scalar(
                 out=th_t[g][:], in0=th_t[g][:], scalar1=ab[:, 1:2], scalar2=ab[:, 0:1], op0=ALU.mult, op1=ALU.add
@@ -201,7 +255,7 @@ def tile_rbm_t_kernel(tc, input_data, W, U, h_bias, y_bias, out):
         def r_transposes(g):
             if g < 0 or g >= NG:
                 return
-            rT = ps_rt.tile([P, T_GRP, P], F32)
+            rT = ps_rt.tile([P, T_GRP, P], F32, tag="rT")
             rt_t[g] = rT
             for tt in range(T_GRP):
                 nc.tensor.transpose(out=rT[:, tt, :], in_=th_t[g][:, tt * P : (tt + 1) * P], identity=ident[:])
@@ -226,35 +280,88 @@ def tile_rbm_t_kernel(tc, input_data, W, U, h_bias, y_bias, out):
                 op=ALU.mult,
             )
 
-        for s in range(NG + 5):
-            for b in range(4):
+        def sums_early():
+            nc.gpsimd.tensor_tensor(
+                out=ssum[:, 0:T_EARLY], in0=prod[:, 0:T_EARLY, 0], in1=prod[:, 0:T_EARLY, 1], op=ALU.add
+            )
+
+        def quotients_early():
+            nc.vector.reciprocal(out=rsum[:, 0:T_EARLY], in_=ssum[:, 0:T_EARLY])
+            nc.gpsimd.tensor_tensor(
+                out=osb[:, 0:T_EARLY, :],
+                in0=prod[:, 0:T_EARLY, :],
+                in1=rsum[:, 0:T_EARLY].unsqueeze(2).to_broadcast([P, T_EARLY, 2]),
+                op=ALU.mult,
+            )
+
+        for s in range(NG):
+            last = s == NG - 1
+            if last:
+                mx(s - 2)
+            for b in (0, 2, 1, 3) if last else range(4):
                 x_transposes(s, b)
-            if s == 0:
-                w_transposes()
+                if s == 0 and b == 0:
+                    w_transposes()
+                    w_quantise()
+                    constants_before_exp()
             load(s + XBUFS)
             r_transposes(s - 4)
-            mx(s - 2)
-
-            if s == 0:
-                w_quantise()
-                constants_before_exp()
+            if not last:
+                mx(s - 2)
             if s == 2:
                 nc.scalar.activation(out=eout[:], in_=ein[:], func=ACT.Exp)
             tanh(s - 3)
-            for b in range(3):
-                copy_out(s, b)
-            if not on_vector(s, 3):
-                copy_out(s, 3)
+            for b in (0, 2, 1, 3) if last else range(4):
+                if not on_vector(s, b):
+                    copy_out(s, b)
+                if last and b == 2:
+                    tanh(s - 2)
 
+            if s == 0:
+                copy_out(0, 1)
+                copy_out(0, 3)
+            if s == 1:
+                copy_out(1, 1)
+                copy_out(1, 3)
             separate(s + 1)
             products(s - 5)
+            if s == NG - 2:
+                sums_early()
+            if last:
+                quotients_early()
             quantise(s - 1)
             if s == 2:
                 constants_after_exp()
             affine(s - 3)
-            if on_vector(s, 3):
-                copy_out(s, 3)
-            if s == NG + 1:
-                normalise(0, T_EARLY)
+
+        g = NG - 1
+        new_codes(g)
+        mx(g - 1)
+        r_transposes(g - 3)
+        tanh(g - 1)
+        quantise_bank(g, 0)
+        quantise_bank(g, 2)
+        affine(g - 2)
+        products(g - 4)
+        pf = ps_xt.tile([P, 2, 256], F32, name="xt")
+        mx_half(g, 0, pf[:, 0, :])
+        r_transposes(g - 2)
+        tanh_half(g, 0)
+        affine_scalar(g - 1)
+        quantise_bank(g, 1)
+        quantise_bank(g, 3)
+        products(g - 3)
+        pf = ps_xt.tile([P, 2, 256], F32, name="xt")
+        mx_half(g, 1, pf[:, 0, :])
+        r_transposes(g - 1)
+        tanh_half(g, 1)
+        affine((g, 0))
+        products(g - 2)
+        r_half(g, 0)
+        affine((g, 1))
+        products(g - 1)
+        r_half(g, 1)
+        products_half(g, 0)
+        products_half(g, 1)
         normalise(T_EARLY, T_ALL)
         nc.sync.dma_start(out=out.rearrange("(p t) c -> p (t c)", t=T_ALL), in_=osb[:].rearrange("p t c -> p (t c)"))

from contextlib import ExitStack

import concourse.mybir as mybir
from concourse.masks import make_identity

F32 = mybir.dt.float32
BF16 = mybir.dt.bfloat16
U32 = mybir.dt.uint32
U8 = mybir.dt.uint8
FP8X4 = mybir.dt.float8_e4m3fn_x4
ACT = mybir.ActivationFunctionType
ALU = mybir.AluOpType
AX = mybir.AxisListType

P = 128
B, NV, NH = 16384, 1024, 128
T_ALL = B // P
T_GRP = 4
NG = T_ALL // T_GRP
COLS = T_GRP * P
PASSES = NV // 512
HALF = NH // 2
XBUFS = 8
T_EARLY = 100
FIRST_SEPARATED = 3
FLOPS = 2 * B * NV * NH


def tile_rbm_t_kernel(tc, input_data, W, U, h_bias, y_bias, out):
    nc = tc.nc
    with ExitStack() as ctx:
        keep = ctx.enter_context(tc.tile_pool(name="keep", bufs=1))
        xpool = ctx.enter_context(tc.tile_pool(name="xpool", bufs=XBUFS))
        spool = ctx.enter_context(tc.tile_pool(name="spool", bufs=3))
        gpool = ctx.enter_context(tc.tile_pool(name="gpool", bufs=3))
        qpool = ctx.enter_context(tc.tile_pool(name="qpool", bufs=4))
        tpool = ctx.enter_context(tc.tile_pool(name="tpool", bufs=4))
        ps_xt = ctx.enter_context(tc.psum_pool(name="ps_xt", bufs=4))
        ps_pf = ctx.enter_context(tc.psum_pool(name="ps_pf", bufs=2))
        ps_rt = ctx.enter_context(tc.psum_pool(name="ps_rt", bufs=2))
        ctx.enter_context(tc.manual_schedule())

        xv = input_data.rearrange("(p t) k -> p (t k)", t=T_ALL)
        sep_t = {}
        xin_t, xt_t, grp_t, codes_t, scl_t, pf_t, th_t, rt_t = {}, {}, {}, {}, {}, {}, {}, {}

        def load(g):
            if g >= NG:
                return
            xin = xpool.tile([P, T_GRP * NV], BF16)
            xin_t[g] = xin
            pieces = T_GRP if g == 0 else 1
            step = T_GRP * NV // pieces
            for i in range(pieces):
                nc.sync.dma_start(
                    out=xin[:, i * step : (i + 1) * step],
                    in_=xv[:, g * T_GRP * NV + i * step : g * T_GRP * NV + (i + 1) * step],
                )

        load(0)
        wsb = keep.tile([P, NV], BF16)
        nc.scalar.dma_start(out=wsb[:], in_=W)
        usb = keep.tile([P, 2], BF16)
        hsb = keep.tile([P, 1], BF16)
        ysb = keep.tile([P, 2], BF16)
        nc.vector.memset(ysb[:], 0.0)
        with nc.allow_non_contiguous_dma(reason="one or two elements a partition"):
            nc.scalar.dma_start(out=usb[:], in_=U)
            nc.scalar.dma_start(out=hsb[:], in_=h_bias.rearrange("o j -> j o"))
            nc.scalar.dma_start(out=ysb[0:1, :], in_=y_bias)
        for g in range(1, XBUFS):
            load(g)

        ident = keep.tile([P, P], F32)
        make_identity(nc, ident[:])

        wgrp = keep.tile([P, PASSES * P * 4], BF16, align_bytes=64)
        wcodes = keep.tile([P, PASSES * P], U32, align_bytes=64)
        wscl = keep.tile([P, PASSES * P], U8, align_bytes=64)
        tb = keep.tile([P, 1], F32)
        usw = keep.tile([P, 2], F32)
        ein = keep.tile([P, 2], F32)
        eout = keep.tile([P, 2], F32)
        ab = keep.tile([P, 2], F32)
        prod = keep.tile([P, T_ALL, 2], F32)
        ssum = keep.tile([P, T_ALL], F32)
        rsum = keep.tile([P, T_ALL], F32)
        osb = keep.tile([P, T_ALL, 2], F32)

        def w_transposes():
            ww = wsb[:].bitcast(F32)
            wt = ps_rt.tile([P, PASSES, 2, P], F32, tag="rT")
            rt_t["w"] = wt
            for gp in range(PASSES):
                for u in range(2):
                    w0 = 256 * gp
                    nc.tensor.transpose(out=wt[:, gp, u, :], in_=ww[:, w0 + u : w0 + 256 : 2], identity=ident[:])

        def w_quantise():
            nc.vector.tensor_copy(
                out=wgrp[:].bitcast(F32).rearrange("p (g j u) -> p g j u", g=PASSES, u=2),
                in_=rt_t["w"][:].rearrange("p g u j -> p g j u"),
            )
            nc.vector.quantize_mx(out=wcodes[:].bitcast(FP8X4), scales=wscl[:], in_=wgrp[:])

        def constants_before_exp():
            nc.vector.tensor_copy(out=usw[0:HALF, 0:1], in_=usb[0:HALF, 1:2])
            nc.vector.tensor_copy(out=usw[0:HALF, 1:2], in_=usb[0:HALF, 0:1])
            nc.vector.tensor_copy(out=usw[HALF:P, :], in_=usb[HALF:P, :])
            nc.vector.tensor_tensor(out=tb[:], in0=hsb[:], in1=usw[:, 0:1], op=ALU.add)
            nc.vector.tensor_scalar_mul(out=tb[:], in0=tb[:], scalar1=0.5)
            nc.vector.tensor_tensor(out=ein[:, 0:1], in0=ysb[:, 0:1], in1=ysb[:, 1:2], op=ALU.subtract)
            nc.vector.tensor_tensor(out=ein[:, 1:2], in0=usw[:, 1:2], in1=usw[:, 0:1], op=ALU.subtract)
            nc.vector.tensor_tensor(out=ein[:, 1:2], in0=ein[:, 1:2], in1=ein[:, 0:1], op=ALU.add)

        def constants_after_exp():
            nc.vector.tensor_tensor(out=ab[:, 0:1], in0=eout[:, 1:2], in1=eout[:, 0:1], op=ALU.add)
            nc.vector.tensor_tensor(out=ab[:, 1:2], in0=eout[:, 1:2], in1=eout[:, 0:1], op=ALU.subtract)
            nc.vector.tensor_scalar_mul(out=ab[:], in0=ab[:], scalar1=0.5)

        def on_vector(g, b):
            return (g == 0 and b in (1, 3)) or (g == 1 and b in (1, 3))

        def n_separated(g):
            return 2 if g >= FIRST_SEPARATED else 0

        def separate(g):
            if g < FIRST_SEPARATED or g >= NG:
                return
            n = n_separated(g)
            sep = spool.tile([P, 2, n * 256], F32, name="sep%d" % n)
            sep_t[g] = sep
            src = xin_t[g][:].bitcast(F32)[:, 0 : n * 512]
            nc.vector.tensor_copy(out=sep[:], in_=src.rearrange("p (b u) -> p u b", u=2))

        def x_transposes(g, b):
            if g < 0 or g >= NG:
                return
            gp, h = b // 2, b % 2
            xw = xin_t[g][:].bitcast(F32)
            xt = ps_xt.tile([P, 2, 256], F32)
            xt_t[(g, b)] = xt
            for tt in range(2):
                for u in range(2):
                    t = 2 * h + tt
                    if t < n_separated(g):
                        win = sep_t[g][:, u, t * 256 + gp * 128 : t * 256 + gp * 128 + 128]
                    else:
                        w0 = t * 512 + 256 * gp
                        win = xw[:, w0 + u : w0 + 256 : 2]
                    nc.tensor.transpose(out=xt[:, u, tt * P : (tt + 1) * P], in_=win, identity=ident[:])

        def copy_out(g, b):
            if g < 0 or g >= NG:
                return
            if g not in grp_t:
                grp = gpool.tile([P, PASSES * COLS * 4], BF16, align_bytes=64)
                grp_t[g] = grp
            o0 = (b // 2) * 1024 + (b % 2) * 512
            dst = grp_t[g][:].bitcast(F32)[:, o0 : o0 + 512].rearrange("p (c u) -> p c u", u=2)
            src = xt_t[(g, b)][:].rearrange("p u c -> p c u")
            if on_vector(g, b):
                nc.vector.tensor_copy(out=dst, in_=src)
            else:
                nc.scalar.copy(out=dst, in_=src)

        def quantise(g):
            if g < 0 or g >= NG:
                return
            new_codes(g)
            nc.vector.quantize_mx(out=codes_t[g][:].bitcast(FP8X4), scales=scl_t[g][:], in_=grp_t[g][:])

        def new_codes(g):
            codes = qpool.tile([P, PASSES * COLS], U32, align_bytes=64)
            scl = qpool.tile([P, PASSES * COLS], U8, align_bytes=64)
            codes_t[g], scl_t[g] = codes, scl

        def quantise_bank(g, b):
            c0 = (b // 2) * COLS + (b % 2) * 256
            nc.vector.quantize_mx(
                out=codes_t[g][:, c0 : c0 + 256].bitcast(FP8X4),
                scales=scl_t[g][:, c0 : c0 + 256],
                in_=grp_t[g][:, 4 * c0 : 4 * c0 + 1024],
            )

        def mx_half(g, h, pf):
            pf_t[(g, h)] = pf
            for gp in range(PASSES):
                c0 = gp * COLS + h * 256
                nc.tensor.matmul_mx(
                    out=pf,
                    lhsT=wcodes[:, gp * P : (gp + 1) * P].bitcast(FP8X4),
                    lhsT_scale=wscl[:, gp * P : (gp + 1) * P],
                    rhs=codes_t[g][:, c0 : c0 + 256].bitcast(FP8X4),
                    rhs_scale=scl_t[g][:, c0 : c0 + 256],
                    start=(gp == 0),
                    stop=(gp == PASSES - 1),
                )

        def tanh_half(g, h):
            th = tpool.tile([P, 256], F32)
            th_t[(g, h)] = th
            nc.scalar.activation(out=th[:], in_=pf_t[(g, h)], func=ACT.Tanh, bias=tb[:, 0:1], scale=0.5)

        def affine_scalar(k):
            nc.scalar.activation(
                out=th_t[k][:], in_=th_t[k][:], func=ACT.Identity, bias=ab[:, 0:1], scale=ab[:, 1:2]
            )

        def r_half(g, h):
            rT = ps_rt.tile([P, 2, P], F32, tag="rT")
            rt_t[(g, h)] = rT
            for tt in range(2):
                nc.tensor.transpose(out=rT[:, tt, :], in_=th_t[(g, h)][:, tt * P : (tt + 1) * P], identity=ident[:])

        def products_half(g, h):
            t0 = g * T_GRP + 2 * h
            nc.vector.tensor_reduce(
                out=prod[:, t0 : t0 + 2, :].rearrange("p t s -> p (t s)"),
                in_=rt_t[(g, h)][:].rearrange("p t (s j) -> p (t s) j", s=2),
                axis=AX.X,
                op=ALU.mult,
            )

        def mx(g):
            if g < 0 or g >= NG:
                return
            pf = ps_pf.tile([P, COLS], F32)
            pf_t[g] = pf
            for gp in range(PASSES):
                nc.tensor.matmul_mx(
                    out=pf[:],
                    lhsT=wcodes[:, gp * P : (gp + 1) * P].bitcast(FP8X4),
                    lhsT_scale=wscl[:, gp * P : (gp + 1) * P],
                    rhs=codes_t[g][:, gp * COLS : (gp + 1) * COLS].bitcast(FP8X4),
                    rhs_scale=scl_t[g][:, gp * COLS : (gp + 1) * COLS],
                    start=(gp == 0),
                    stop=(gp == PASSES - 1),
                )

        def tanh(g):
            if g < 0 or g >= NG:
                return
            th = tpool.tile([P, COLS], F32)
            th_t[g] = th
            nc.scalar.activation(out=th[:], in_=pf_t[g][:], func=ACT.Tanh, bias=tb[:, 0:1], scale=0.5)

        def affine(g):
            if g not in th_t:
                return
            nc.vector.tensor_scalar(
                out=th_t[g][:], in0=th_t[g][:], scalar1=ab[:, 1:2], scalar2=ab[:, 0:1], op0=ALU.mult, op1=ALU.add
            )

        def r_transposes(g):
            if g < 0 or g >= NG:
                return
            rT = ps_rt.tile([P, T_GRP, P], F32, tag="rT")
            rt_t[g] = rT
            for tt in range(T_GRP):
                nc.tensor.transpose(out=rT[:, tt, :], in_=th_t[g][:, tt * P : (tt + 1) * P], identity=ident[:])

        def products(g):
            if g < 0 or g >= NG:
                return
            nc.vector.tensor_reduce(
                out=prod[:, g * T_GRP : (g + 1) * T_GRP, :].rearrange("p t s -> p (t s)"),
                in_=rt_t[g][:].rearrange("p t (s j) -> p (t s) j", s=2),
                axis=AX.X,
                op=ALU.mult,
            )

        def normalise(t0, t1):
            nc.vector.tensor_reduce(out=ssum[:, t0:t1], in_=prod[:, t0:t1, :], axis=AX.X, op=ALU.add)
            nc.vector.reciprocal(out=rsum[:, t0:t1], in_=ssum[:, t0:t1])
            nc.vector.tensor_tensor(
                out=osb[:, t0:t1, :],
                in0=prod[:, t0:t1, :],
                in1=rsum[:, t0:t1].unsqueeze(2).to_broadcast([P, t1 - t0, 2]),
                op=ALU.mult,
            )

        def sums_early():
            nc.gpsimd.tensor_tensor(
                out=ssum[:, 0:T_EARLY], in0=prod[:, 0:T_EARLY, 0], in1=prod[:, 0:T_EARLY, 1], op=ALU.add
            )

        def quotients_early():
            nc.vector.reciprocal(out=rsum[:, 0:T_EARLY], in_=ssum[:, 0:T_EARLY])
            nc.gpsimd.tensor_tensor(
                out=osb[:, 0:T_EARLY, :],
                in0=prod[:, 0:T_EARLY, :],
                in1=rsum[:, 0:T_EARLY].unsqueeze(2).to_broadcast([P, T_EARLY, 2]),
                op=ALU.mult,
            )

        for s in range(NG):
            last = s == NG - 1
            if last:
                mx(s - 2)
            for b in (0, 2, 1, 3) if last else range(4):
                x_transposes(s, b)
                if s == 0 and b == 0:
                    w_transposes()
                    w_quantise()
                    constants_before_exp()
            load(s + XBUFS)
            r_transposes(s - 4)
            if not last:
                mx(s - 2)
            if s == 2:
                nc.scalar.activation(out=eout[:], in_=ein[:], func=ACT.Exp)
            tanh(s - 3)
            for b in (0, 2, 1, 3) if last else range(4):
                if not on_vector(s, b):
                    copy_out(s, b)
                if last and b == 2:
                    tanh(s - 2)

            if s == 0:
                copy_out(0, 1)
                copy_out(0, 3)
            if s == 1:
                copy_out(1, 1)
                copy_out(1, 3)
            separate(s + 1)
            products(s - 5)
            if s == NG - 2:
                sums_early()
            if last:
                quotients_early()
            quantise(s - 1)
            if s == 2:
                constants_after_exp()
            affine(s - 3)

        g = NG - 1
        new_codes(g)
        mx(g - 1)
        r_transposes(g - 3)
        tanh(g - 1)
        quantise_bank(g, 0)
        quantise_bank(g, 2)
        affine(g - 2)
        products(g - 4)
        pf = ps_xt.tile([P, 2, 256], F32, name="xt")
        mx_half(g, 0, pf[:, 0, :])
        r_transposes(g - 2)
        tanh_half(g, 0)
        affine_scalar(g - 1)
        quantise_bank(g, 1)
        quantise_bank(g, 3)
        products(g - 3)
        pf = ps_xt.tile([P, 2, 256], F32, name="xt")
        mx_half(g, 1, pf[:, 0, :])
        r_transposes(g - 1)
        tanh_half(g, 1)
        affine((g, 0))
        products(g - 2)
        r_half(g, 0)
        affine((g, 1))
        products(g - 1)
        r_half(g, 1)
        products_half(g, 0)
        products_half(g, 1)
        normalise(T_EARLY, T_ALL)
        nc.sync.dma_start(out=out.rearrange("(p t) c -> p (t c)", t=T_ALL), in_=osb[:].rearrange("p t c -> p (t c)"))
